import numpy as np
import ml_dtypes


def mxq(x, axis, fmt="e4m3"):
    dtype, down = {"e4m3": (ml_dtypes.float8_e4m3fn, 7), "e5m2": (ml_dtypes.float8_e5m2, 14)}[fmt]
    v = np.moveaxis(np.asarray(x, np.float32).astype(ml_dtypes.bfloat16).astype(np.float64), axis, -1)
    blocks = v.reshape(v.shape[:-1] + (-1, 32))
    amax = np.abs(blocks).max(-1, keepdims=True)
    byte = np.maximum(np.where(amax > 0, np.frexp(amax)[1] - 1 + 127, 0) - down, 1)
    scale = np.exp2(byte - 127.0)
    codes = (blocks / scale).astype(np.float32).astype(dtype).astype(np.float64)
    return np.moveaxis((codes * scale).reshape(v.shape), -1, axis)


WIDE = False


def mx_kscale(k):
    if not WIDE:
        return np.ones(k)
    levels = np.array([10, -10, 5, -5, 0])
    a = np.random.permutation(np.resize(levels, k // 512 * 4)).reshape(k // 512, 4)
    idx = np.arange(k)
    return np.exp2(a[idx // 512, idx % 128 // 32])


BF16 = ml_dtypes.bfloat16


def bf(x):
    return np.asarray(x, np.float32).astype(BF16)


def f64(x):
    return np.asarray(x).astype(np.float64)


T, K, E, H, KVH, D = 128, 1024, 512, 16, 4, 128
EPS = 1e-05


def rmsnorm(x, w):
    var = np.mean(np.square(x), axis=-1, keepdims=True)
    return x * (1.0 / np.sqrt(var + EPS)) * w


def setup_inputs():
    s = mx_kscale(E)
    return {"hidden_states": bf(np.random.standard_normal((T, E)) * s),
            "Wq": bf(np.random.standard_normal((H * D, E)) / np.sqrt(E) / s),
            "q_norm_w": bf(1.5 + 0.1 * np.random.standard_normal(D))}


def reference(hidden_states, Wq, q_norm_w):
    q = mxq(f64(hidden_states), 1, "e4m3") @ mxq(f64(Wq), 1, "e4m3").T
    qh = rmsnorm(q.reshape(T, H, D), f64(q_norm_w))
    return qh.transpose(1, 0, 2)

@@ -1,0 +1,133 @@
+from contextlib import ExitStack
+
+import concourse.masks as masks
+import concourse.mybir as mybir
+
+F32 = mybir.dt.float32
+BF16 = mybir.dt.bfloat16
+U32 = mybir.dt.uint32
+U8 = mybir.dt.uint8
+FP8X4 = mybir.dt.float8_e4m3fn_x4
+ACT = mybir.ActivationFunctionType
+ALU = mybir.AluOpType
+
+P = 128
+TOKENS = 128
+K = 512
+HEADS = 16
+HEAD_DIM = 128
+EPS = 1e-05
+
+K_WORDS = K // 2
+HALVES = K_WORDS // P
+CHUNK = 512
+N_CHUNKS = HEADS * HEAD_DIM // CHUNK
+ROWS = CHUNK // P
+HEADS_PER_CHUNK = CHUNK // HEAD_DIM
+ROWS_PER_BANK = 2
+
+FLOPS = 2 * TOKENS * HEADS * HEAD_DIM * K
+
+
+def tile_combcrossattention_pa_s_kernel(tc, hidden_states, Wq, q_norm_w, out):
+    nc = tc.nc
+    with ExitStack() as ctx:
+        consts = ctx.enter_context(tc.tile_pool(name="consts", bufs=1))
+        chunks = ctx.enter_context(tc.tile_pool(name="chunks", bufs=N_CHUNKS))
+        flipped = ctx.enter_context(tc.psum_pool(name="flipped", bufs=4))
+        sums = ctx.enter_context(tc.psum_pool(name="sums", bufs=3))
+
+        hs_raw = consts.tile([P, K], BF16)
+        nc.sync.dma_start(out=hs_raw[:], in_=hidden_states)
+        w_raw = []
+        for j in range(N_CHUNKS):
+            raw = chunks.tile([P, ROWS * K], BF16, name="w_raw")
+            rows = Wq[j * CHUNK : (j + 1) * CHUNK, :]
+            nc.sync.dma_start(out=raw[:], in_=rows.rearrange("(p a) k -> p (a k)", a=ROWS))
+            w_raw.append(raw)
+        gain = consts.tile([P, HEAD_DIM], BF16)
+        nc.scalar.dma_start(out=gain[:], in_=q_norm_w.partition_broadcast(P))
+
+        ident = consts.tile([P, P], F32)
+        masks.make_identity(nc, ident[:])
+        one = consts.tile([P, 1], F32)
+        nc.vector.memset(one[:], 1.0)
+        nc.scalar.activation(out=one[:], in_=one[:], func=ACT.Sqrt)
+
+        def transpose_words(dst, src_words):
+            for u in range(HALVES):
+                nc.tensor.transpose(dst[:, u, :], src_words[:, u * P : (u + 1) * P], ident[:])
+
+        hs_flipped = flipped.tile([P, HALVES, TOKENS], F32, name="hs_flipped", tag="bank")
+        transpose_words(hs_flipped, hs_raw[:].bitcast(F32))
+        hs_grouped = consts.tile([P, TOKENS * 4], BF16, align_bytes=64)
+        nc.vector.tensor_copy(
+            out=hs_grouped[:].bitcast(F32).rearrange("p (r u) -> p r u", u=HALVES),
+            in_=hs_flipped[:].rearrange("p u r -> p r u"),
+        )
+        hs_codes = consts.tile([P, TOKENS], U32, align_bytes=64)
+        hs_scales = consts.tile([P, TOKENS], U8, align_bytes=64)
+        nc.vector.quantize_mx(out=hs_codes[:].bitcast(FP8X4), scales=hs_scales[:], in_=hs_grouped[:])
+
+        for j in range(N_CHUNKS):
+            words = w_raw[j][:].bitcast(F32)
+            grouped = chunks.tile([P, CHUNK * 4], BF16, align_bytes=64, name="grouped")
+            grouped_words = grouped[:].bitcast(F32).rearrange(
+                "p (a c u) -> p a c u", a=ROWS, u=HALVES
+            )
+            for b in range(ROWS // ROWS_PER_BANK):
+                bank = flipped.tile([P, ROWS_PER_BANK, HALVES, P], F32, name="bank", tag="bank")
+                for i in range(ROWS_PER_BANK):
+                    a = b * ROWS_PER_BANK + i
+                    transpose_words(bank[:, i], words[:, a * K_WORDS : (a + 1) * K_WORDS])
+                dst = grouped_words[:, b * ROWS_PER_BANK : (b + 1) * ROWS_PER_BANK]
+                src = bank[:].rearrange("p a u c -> p a c u")
+                if b == 0:
+                    nc.scalar.copy(out=dst, in_=src)
+                else:
+                    nc.vector.tensor_copy(out=dst, in_=src)
+
+            codes = chunks.tile([P, CHUNK], U32, align_bytes=64, name="codes")
+            scales = chunks.tile([P, CHUNK], U8, align_bytes=64, name="scales")
+            nc.vector.quantize_mx(out=codes[:].bitcast(FP8X4), scales=scales[:], in_=grouped[:])
+            acc = sums.tile([TOKENS, CHUNK], F32, name="acc")
+            nc.tensor.matmul_mx(
+                out=acc[:],
+                lhsT=hs_codes[:].bitcast(FP8X4),
+                lhsT_scale=hs_scales[:],
+                rhs=codes[:].bitcast(FP8X4),
+                rhs_scale=scales[:],
+                start=True,
+                stop=True,
+            )
+
+            squares = chunks.tile([TOKENS, HEADS_PER_CHUNK, ROWS, P // ROWS], F32, name="squares")
+            sumsq = chunks.tile([TOKENS, HEADS_PER_CHUNK], F32, name="sumsq")
+            acc_heads = acc[:].rearrange("t (a h c) -> t h a c", a=ROWS, h=HEADS_PER_CHUNK)
+            for h in range(HEADS_PER_CHUNK):
+                nc.scalar.activation(
+                    out=squares[:, h],
+                    in_=acc_heads[:, h],
+                    func=ACT.Square,
+                    accum_out=sumsq[:, h : h + 1],
+                )
+            rms = chunks.tile([TOKENS, HEADS_PER_CHUNK], F32, name="rms")
+            nc.scalar.activation(
+                out=rms[:], in_=sumsq[:], func=ACT.Sqrt, scale=1.0 / HEAD_DIM, bias=EPS
+            )
+            inv_rms = chunks.tile([TOKENS, HEADS_PER_CHUNK], F32, name="inv_rms")
+            nc.vector.reciprocal(out=inv_rms[:], in_=rms[:])
+
+            normed = chunks.tile([TOKENS, HEADS_PER_CHUNK, HEAD_DIM], F32, name="normed")
+            acc_by_d = acc[:].rearrange("t (a h c) -> t h c a", a=ROWS, h=HEADS_PER_CHUNK)
+            for h in range(HEADS_PER_CHUNK):
+                nc.vector.scalar_tensor_tensor(
+                    out=normed[:, h, :].rearrange("t (c a) -> t c a", a=ROWS),
+                    in0=acc_by_d[:, h],
+                    scalar=inv_rms[:, h : h + 1],
+                    in1=gain[:].rearrange("t (c a) -> t c a", a=ROWS),
+                    op0=ALU.mult,
+                    op1=ALU.mult,
+                )
+            heads = out[j * HEADS_PER_CHUNK : (j + 1) * HEADS_PER_CHUNK]
+            nc.sync.dma_start(out=heads.rearrange("h t d -> t h d"), in_=normed[:])

@@ -45,14 +45,22 @@ def tile_combcrossattention_pa_s_kernel(tc, hidden_states, Wq, q_norm_w, out):
             rows = Wq[j * CHUNK : (j + 1) * CHUNK, :]
             nc.sync.dma_start(out=raw[:], in_=rows.rearrange("(p a) k -> p (a k)", a=ROWS))
             w_raw.append(raw)
-        gain = consts.tile([P, HEAD_DIM], BF16)
-        nc.scalar.dma_start(out=gain[:], in_=q_norm_w.partition_broadcast(P))
+        gain_row = consts.tile([P, HEAD_DIM], BF16)
+        nc.vector.memset(gain_row[:], 0.0)
+        nc.scalar.dma_start(out=gain_row[0:1, :], in_=q_norm_w.rearrange("(o d) -> o d", o=1))
 
         ident = consts.tile([P, P], F32)
         masks.make_identity(nc, ident[:])
         one = consts.tile([P, 1], F32)
         nc.vector.memset(one[:], 1.0)
         nc.scalar.activation(out=one[:], in_=one[:], func=ACT.Sqrt)
+
+        ones = consts.tile([P, P], BF16)
+        nc.vector.memset(ones[:], 1.0)
+        gain_spread = flipped.tile([P, HEAD_DIM], F32, name="gain_spread", tag="bank")
+        nc.tensor.matmul(out=gain_spread[:], lhsT=ones[:], rhs=gain_row[:], start=True, stop=True)
+        gain = consts.tile([P, HEAD_DIM], F32)
+        nc.vector.tensor_copy(out=gain[:], in_=gain_spread[:])
 
         def transpose_words(dst, src_words):
             for u in range(HALVES):

@@ -20,11 +20,12 @@ EPS = 1e-05
 
 K_WORDS = K // 2
 HALVES = K_WORDS // P
-CHUNK = 512
-N_CHUNKS = HEADS * HEAD_DIM // CHUNK
-ROWS = CHUNK // P
-HEADS_PER_CHUNK = CHUNK // HEAD_DIM
-ROWS_PER_BANK = 2
+PACK = 4
+PIECE = 256
+N_PIECES = HEADS * HEAD_DIM // PIECE
+ROWS = PIECE // P
+HEADS_PER_PIECE = PIECE // HEAD_DIM
+VECTOR_EVERY = 4
 
 FLOPS = 2 * TOKENS * HEADS * HEAD_DIM * K
 
@@ -33,16 +34,16 @@ def tile_combcrossattention_pa_s_kernel(tc, hidden_states, Wq, q_norm_w, out):
     nc = tc.nc
     with ExitStack() as ctx:
         consts = ctx.enter_context(tc.tile_pool(name="consts", bufs=1))
-        chunks = ctx.enter_context(tc.tile_pool(name="chunks", bufs=N_CHUNKS))
+        pieces = ctx.enter_context(tc.tile_pool(name="pieces", bufs=N_PIECES))
         flipped = ctx.enter_context(tc.psum_pool(name="flipped", bufs=4))
-        sums = ctx.enter_context(tc.psum_pool(name="sums", bufs=3))
+        sums = ctx.enter_context(tc.psum_pool(name="sums", bufs=4))
 
         hs_raw = consts.tile([P, K], BF16)
         nc.sync.dma_start(out=hs_raw[:], in_=hidden_states)
         w_raw = []
-        for j in range(N_CHUNKS):
-            raw = chunks.tile([P, ROWS * K], BF16, name="w_raw")
-            rows = Wq[j * CHUNK : (j + 1) * CHUNK, :]
+        for i in range(N_PIECES):
+            raw = pieces.tile([P, ROWS * K], BF16, name="w_raw")
+            rows = Wq[i * PIECE : (i + 1) * PIECE, :]
             nc.sync.dma_start(out=raw[:], in_=rows.rearrange("(p a) k -> p (a k)", a=ROWS))
             w_raw.append(raw)
         gain_row = consts.tile([P, HEAD_DIM], BF16)
@@ -51,16 +52,11 @@ def tile_combcrossattention_pa_s_kernel(tc, hidden_states, Wq, q_norm_w, out):
 
         ident = consts.tile([P, P], F32)
         masks.make_identity(nc, ident[:])
+        ones = consts.tile([P, P], BF16)
+        nc.vector.memset(ones[:], 1.0)
         one = consts.tile([P, 1], F32)
         nc.vector.memset(one[:], 1.0)
         nc.scalar.activation(out=one[:], in_=one[:], func=ACT.Sqrt)
-
-        ones = consts.tile([P, P], BF16)
-        nc.vector.memset(ones[:], 1.0)
-        gain_spread = flipped.tile([P, HEAD_DIM], F32, name="gain_spread", tag="bank")
-        nc.tensor.matmul(out=gain_spread[:], lhsT=ones[:], rhs=gain_row[:], start=True, stop=True)
-        gain = consts.tile([P, HEAD_DIM], F32)
-        nc.vector.tensor_copy(out=gain[:], in_=gain_spread[:])
 
         def transpose_words(dst, src_words):
             for u in range(HALVES):
@@ -68,7 +64,7 @@ def tile_combcrossattention_pa_s_kernel(tc, hidden_states, Wq, q_norm_w, out):
 
         hs_flipped = flipped.tile([P, HALVES, TOKENS], F32, name="hs_flipped", tag="bank")
         transpose_words(hs_flipped, hs_raw[:].bitcast(F32))
-        hs_grouped = consts.tile([P, TOKENS * 4], BF16, align_bytes=64)
+        hs_grouped = consts.tile([P, TOKENS * PACK], BF16, align_bytes=64)
         nc.vector.tensor_copy(
             out=hs_grouped[:].bitcast(F32).rearrange("p (r u) -> p r u", u=HALVES),
             in_=hs_flipped[:].rearrange("p u r -> p r u"),
@@ -77,65 +73,101 @@ def tile_combcrossattention_pa_s_kernel(tc, hidden_states, Wq, q_norm_w, out):
         hs_scales = consts.tile([P, TOKENS], U8, align_bytes=64)
         nc.vector.quantize_mx(out=hs_codes[:].bitcast(FP8X4), scales=hs_scales[:], in_=hs_grouped[:])
 
-        for j in range(N_CHUNKS):
-            words = w_raw[j][:].bitcast(F32)
-            grouped = chunks.tile([P, CHUNK * 4], BF16, align_bytes=64, name="grouped")
-            grouped_words = grouped[:].bitcast(F32).rearrange(
-                "p (a c u) -> p a c u", a=ROWS, u=HALVES
-            )
-            for b in range(ROWS // ROWS_PER_BANK):
-                bank = flipped.tile([P, ROWS_PER_BANK, HALVES, P], F32, name="bank", tag="bank")
-                for i in range(ROWS_PER_BANK):
-                    a = b * ROWS_PER_BANK + i
-                    transpose_words(bank[:, i], words[:, a * K_WORDS : (a + 1) * K_WORDS])
-                dst = grouped_words[:, b * ROWS_PER_BANK : (b + 1) * ROWS_PER_BANK]
-                src = bank[:].rearrange("p a u c -> p a c u")
-                if b == 0:
-                    nc.scalar.copy(out=dst, in_=src)
-                else:
-                    nc.vector.tensor_copy(out=dst, in_=src)
+        gain = consts.tile([P, HEAD_DIM], F32)
 
-            codes = chunks.tile([P, CHUNK], U32, align_bytes=64, name="codes")
-            scales = chunks.tile([P, CHUNK], U8, align_bytes=64, name="scales")
-            nc.vector.quantize_mx(out=codes[:].bitcast(FP8X4), scales=scales[:], in_=grouped[:])
-            acc = sums.tile([TOKENS, CHUNK], F32, name="acc")
+        def spread_gain():
+            gain_spread = flipped.tile([P, HEAD_DIM], F32, name="gain_spread", tag="bank")
+            nc.tensor.matmul(out=gain_spread[:], lhsT=ones[:], rhs=gain_row[:], start=True, stop=True)
+            nc.vector.tensor_copy(out=gain[:], in_=gain_spread[:])
+
+        banks = {}
+        grouped = {}
+        codes = {}
+        scales = {}
+        acc = {}
+        inv_rms = {}
+
+        def flip(i):
+            words = w_raw[i][:].bitcast(F32)
+            banks[i] = flipped.tile([P, ROWS, HALVES, P], F32, name="bank", tag="bank")
+            for a in range(ROWS):
+                transpose_words(banks[i][:, a], words[:, a * K_WORDS : (a + 1) * K_WORDS])
+
+        def regroup(i):
+            grouped[i] = pieces.tile([P, PIECE * PACK], BF16, align_bytes=64, name="grouped")
+            dst = grouped[i][:].bitcast(F32).rearrange("p (a c u) -> p a c u", a=ROWS, u=HALVES)
+            src = banks[i][:].rearrange("p a u c -> p a c u")
+            if i % VECTOR_EVERY == VECTOR_EVERY - 1:
+                nc.vector.tensor_copy(out=dst, in_=src)
+            else:
+                nc.scalar.copy(out=dst, in_=src)
+
+        def quantise(i):
+            codes[i] = pieces.tile([P, PIECE], U32, align_bytes=64, name="codes")
+            scales[i] = pieces.tile([P, PIECE], U8, align_bytes=64, name="scales")
+            nc.vector.quantize_mx(
+                out=codes[i][:].bitcast(FP8X4), scales=scales[i][:], in_=grouped[i][:]
+            )
+
+        def multiply(i):
+            acc[i] = sums.tile([TOKENS, PIECE], F32, name="acc")
             nc.tensor.matmul_mx(
-                out=acc[:],
+                out=acc[i][:],
                 lhsT=hs_codes[:].bitcast(FP8X4),
                 lhsT_scale=hs_scales[:],
-                rhs=codes[:].bitcast(FP8X4),
-                rhs_scale=scales[:],
+                rhs=codes[i][:].bitcast(FP8X4),
+                rhs_scale=scales[i][:],
                 start=True,
                 stop=True,
             )
 
-            squares = chunks.tile([TOKENS, HEADS_PER_CHUNK, ROWS, P // ROWS], F32, name="squares")
-            sumsq = chunks.tile([TOKENS, HEADS_PER_CHUNK], F32, name="sumsq")
-            acc_heads = acc[:].rearrange("t (a h c) -> t h a c", a=ROWS, h=HEADS_PER_CHUNK)
-            for h in range(HEADS_PER_CHUNK):
+        def mean_square(i):
+            squares = pieces.tile([TOKENS, HEADS_PER_PIECE, ROWS, P // ROWS], F32, name="squares")
+            sumsq = pieces.tile([TOKENS, HEADS_PER_PIECE], F32, name="sumsq")
+            acc_heads = acc[i][:].rearrange("t (a h c) -> t h a c", a=ROWS, h=HEADS_PER_PIECE)
+            for h in range(HEADS_PER_PIECE):
                 nc.scalar.activation(
                     out=squares[:, h],
                     in_=acc_heads[:, h],
                     func=ACT.Square,
                     accum_out=sumsq[:, h : h + 1],
                 )
-            rms = chunks.tile([TOKENS, HEADS_PER_CHUNK], F32, name="rms")
+            rms = pieces.tile([TOKENS, HEADS_PER_PIECE], F32, name="rms")
             nc.scalar.activation(
                 out=rms[:], in_=sumsq[:], func=ACT.Sqrt, scale=1.0 / HEAD_DIM, bias=EPS
             )
-            inv_rms = chunks.tile([TOKENS, HEADS_PER_CHUNK], F32, name="inv_rms")
-            nc.vector.reciprocal(out=inv_rms[:], in_=rms[:])
+            return rms
 
-            normed = chunks.tile([TOKENS, HEADS_PER_CHUNK, HEAD_DIM], F32, name="normed")
-            acc_by_d = acc[:].rearrange("t (a h c) -> t h c a", a=ROWS, h=HEADS_PER_CHUNK)
-            for h in range(HEADS_PER_CHUNK):
+        def normalise(i, rms):
+            inv_rms[i] = pieces.tile([TOKENS, HEADS_PER_PIECE], F32, name="inv_rms")
+            nc.vector.reciprocal(out=inv_rms[i][:], in_=rms[:])
+            normed = pieces.tile([TOKENS, HEADS_PER_PIECE, HEAD_DIM], F32, name="normed")
+            acc_by_d = acc[i][:].rearrange("t (a h c) -> t h c a", a=ROWS, h=HEADS_PER_PIECE)
+            for h in range(HEADS_PER_PIECE):
                 nc.vector.scalar_tensor_tensor(
                     out=normed[:, h, :].rearrange("t (c a) -> t c a", a=ROWS),
                     in0=acc_by_d[:, h],
-                    scalar=inv_rms[:, h : h + 1],
+                    scalar=inv_rms[i][:, h : h + 1],
                     in1=gain[:].rearrange("t (c a) -> t c a", a=ROWS),
                     op0=ALU.mult,
                     op1=ALU.mult,
                 )
-            heads = out[j * HEADS_PER_CHUNK : (j + 1) * HEADS_PER_CHUNK]
+            heads = out[i * HEADS_PER_PIECE : (i + 1) * HEADS_PER_PIECE]
             nc.sync.dma_start(out=heads.rearrange("h t d -> t h d"), in_=normed[:])
+
+        rms_of = {}
+        for step in range(N_PIECES + 4):
+            if step < N_PIECES:
+                flip(step)
+            if step == 3:
+                spread_gain()
+            if 0 <= step - 1 < N_PIECES:
+                regroup(step - 1)
+            if 0 <= step - 4 < N_PIECES:
+                normalise(step - 4, rms_of[step - 4])
+            if 0 <= step - 1 < N_PIECES:
+                quantise(step - 1)
+            if 0 <= step - 2 < N_PIECES:
+                multiply(step - 2)
+            if 0 <= step - 3 < N_PIECES:
+                rms_of[step - 3] = mean_square(step - 3)

@@ -27,6 +27,8 @@ ROWS = PIECE // P
 HEADS_PER_PIECE = PIECE // HEAD_DIM
 VECTOR_EVERY = 4
 
+WARM_PASSES = 16
+
 FLOPS = 2 * TOKENS * HEADS * HEAD_DIM * K
 
 
@@ -37,6 +39,23 @@ def tile_combcrossattention_pa_s_kernel(tc, hidden_states, Wq, q_norm_w, out):
         pieces = ctx.enter_context(tc.tile_pool(name="pieces", bufs=N_PIECES))
         flipped = ctx.enter_context(tc.psum_pool(name="flipped", bufs=4))
         sums = ctx.enter_context(tc.psum_pool(name="sums", bufs=4))
+
+        zeros = consts.tile([P, P * PACK], BF16, align_bytes=64)
+        nc.vector.memset(zeros[:], 0.0)
+        zero_codes = consts.tile([P, P], U32, align_bytes=64)
+        zero_scales = consts.tile([P, P], U8, align_bytes=64)
+        nc.vector.quantize_mx(out=zero_codes[:].bitcast(FP8X4), scales=zero_scales[:], in_=zeros[:])
+        zero_sums = sums.tile([P, P], F32, name="zero_sums", tag="acc")
+        for n in range(WARM_PASSES):
+            nc.tensor.matmul_mx(
+                out=zero_sums[:],
+                lhsT=zero_codes[:].bitcast(FP8X4),
+                lhsT_scale=zero_scales[:],
+                rhs=zero_codes[:].bitcast(FP8X4),
+                rhs_scale=zero_scales[:],
+                start=True,
+                stop=True,
+            )
 
         hs_raw = consts.tile([P, K], BF16)
         nc.sync.dma_start(out=hs_raw[:], in_=hidden_states)
@@ -110,7 +129,7 @@ def tile_combcrossattention_pa_s_kernel(tc, hidden_states, Wq, q_norm_w, out):
             )
 
         def multiply(i):
-            acc[i] = sums.tile([TOKENS, PIECE], F32, name="acc")
+            acc[i] = sums.tile([TOKENS, PIECE], F32, name="acc", tag="acc")
             nc.tensor.matmul_mx(
                 out=acc[i][:],
                 lhsT=hs_codes[:].bitcast(FP8X4),

@@ -25,9 +25,7 @@ PIECE = 256
 N_PIECES = HEADS * HEAD_DIM // PIECE
 ROWS = PIECE // P
 HEADS_PER_PIECE = PIECE // HEAD_DIM
-VECTOR_EVERY = 4
-
-WARM_PASSES = 16
+VECTOR_EVERY = 3
 
 FLOPS = 2 * TOKENS * HEADS * HEAD_DIM * K
 
@@ -40,34 +38,20 @@ def tile_combcrossattention_pa_s_kernel(tc, hidden_states, Wq, q_norm_w, out):
         flipped = ctx.enter_context(tc.psum_pool(name="flipped", bufs=4))
         sums = ctx.enter_context(tc.psum_pool(name="sums", bufs=4))
 
-        zeros = consts.tile([P, P * PACK], BF16, align_bytes=64)
-        nc.vector.memset(zeros[:], 0.0)
-        zero_codes = consts.tile([P, P], U32, align_bytes=64)
-        zero_scales = consts.tile([P, P], U8, align_bytes=64)
-        nc.vector.quantize_mx(out=zero_codes[:].bitcast(FP8X4), scales=zero_scales[:], in_=zeros[:])
-        zero_sums = sums.tile([P, P], F32, name="zero_sums", tag="acc")
-        for n in range(WARM_PASSES):
-            nc.tensor.matmul_mx(
-                out=zero_sums[:],
-                lhsT=zero_codes[:].bitcast(FP8X4),
-                lhsT_scale=zero_scales[:],
-                rhs=zero_codes[:].bitcast(FP8X4),
-                rhs_scale=zero_scales[:],
-                start=True,
-                stop=True,
-            )
-
-        hs_raw = consts.tile([P, K], BF16)
-        nc.sync.dma_start(out=hs_raw[:], in_=hidden_states)
-        w_raw = []
-        for i in range(N_PIECES):
+        def load_piece(i):
             raw = pieces.tile([P, ROWS * K], BF16, name="w_raw")
             rows = Wq[i * PIECE : (i + 1) * PIECE, :]
             nc.sync.dma_start(out=raw[:], in_=rows.rearrange("(p a) k -> p (a k)", a=ROWS))
-            w_raw.append(raw)
+            return raw
+
+        w_raw = [load_piece(0)]
+        hs_raw = consts.tile([P, K], BF16)
+        nc.sync.dma_start(out=hs_raw[:], in_=hidden_states)
         gain_row = consts.tile([P, HEAD_DIM], BF16)
         nc.vector.memset(gain_row[:], 0.0)
-        nc.scalar.dma_start(out=gain_row[0:1, :], in_=q_norm_w.rearrange("(o d) -> o d", o=1))
+        nc.sync.dma_start(out=gain_row[0:1, :], in_=q_norm_w.rearrange("(o d) -> o d", o=1))
+        for i in range(1, N_PIECES):
+            w_raw.append(load_piece(i))
 
         ident = consts.tile([P, P], F32)
         masks.make_identity(nc, ident[:])
@@ -75,11 +59,20 @@ def tile_combcrossattention_pa_s_kernel(tc, hidden_states, Wq, q_norm_w, out):
         nc.vector.memset(ones[:], 1.0)
         one = consts.tile([P, 1], F32)
         nc.vector.memset(one[:], 1.0)
-        nc.scalar.activation(out=one[:], in_=one[:], func=ACT.Sqrt)
+        nc.scalar.activation(out=one[:], in_=one[:], func=ACT.Abs_reciprocal_sqrt)
 
         def transpose_words(dst, src_words):
             for u in range(HALVES):
                 nc.tensor.transpose(dst[:, u, :], src_words[:, u * P : (u + 1) * P], ident[:])
+
+        def flip(i):
+            words = w_raw[i][:].bitcast(F32)
+            bank = flipped.tile([P, ROWS, HALVES, P], F32, name="bank", tag="bank")
+            for a in range(ROWS):
+                transpose_words(bank[:, a], words[:, a * K_WORDS : (a + 1) * K_WORDS])
+            return bank
+
+        bank_of = {0: flip(0)}
 
         hs_flipped = flipped.tile([P, HALVES, TOKENS], F32, name="hs_flipped", tag="bank")
         transpose_words(hs_flipped, hs_raw[:].bitcast(F32))
@@ -92,58 +85,41 @@ def tile_combcrossattention_pa_s_kernel(tc, hidden_states, Wq, q_norm_w, out):
         hs_scales = consts.tile([P, TOKENS], U8, align_bytes=64)
         nc.vector.quantize_mx(out=hs_codes[:].bitcast(FP8X4), scales=hs_scales[:], in_=hs_grouped[:])
 
+        gain_spread = flipped.tile([P, HEAD_DIM], F32, name="gain_spread", tag="bank")
+        nc.tensor.matmul(out=gain_spread[:], lhsT=ones[:], rhs=gain_row[:], start=True, stop=True)
         gain = consts.tile([P, HEAD_DIM], F32)
+        nc.vector.tensor_copy(out=gain[:], in_=gain_spread[:])
 
-        def spread_gain():
-            gain_spread = flipped.tile([P, HEAD_DIM], F32, name="gain_spread", tag="bank")
-            nc.tensor.matmul(out=gain_spread[:], lhsT=ones[:], rhs=gain_row[:], start=True, stop=True)
-            nc.vector.tensor_copy(out=gain[:], in_=gain_spread[:])
+        for i in range(N_PIECES):
+            if i + 1 < N_PIECES:
+                bank_of[i + 1] = flip(i + 1)
 
-        banks = {}
-        grouped = {}
-        codes = {}
-        scales = {}
-        acc = {}
-        inv_rms = {}
-
-        def flip(i):
-            words = w_raw[i][:].bitcast(F32)
-            banks[i] = flipped.tile([P, ROWS, HALVES, P], F32, name="bank", tag="bank")
-            for a in range(ROWS):
-                transpose_words(banks[i][:, a], words[:, a * K_WORDS : (a + 1) * K_WORDS])
-
-        def regroup(i):
-            grouped[i] = pieces.tile([P, PIECE * PACK], BF16, align_bytes=64, name="grouped")
-            dst = grouped[i][:].bitcast(F32).rearrange("p (a c u) -> p a c u", a=ROWS, u=HALVES)
-            src = banks[i][:].rearrange("p a u c -> p a c u")
-            if i % VECTOR_EVERY == VECTOR_EVERY - 1:
+            grouped = pieces.tile([P, PIECE * PACK], BF16, align_bytes=64, name="grouped")
+            dst = grouped[:].bitcast(F32).rearrange("p (a c u) -> p a c u", a=ROWS, u=HALVES)
+            src = bank_of[i][:].rearrange("p a u c -> p a c u")
+            if i % VECTOR_EVERY == 1:
                 nc.vector.tensor_copy(out=dst, in_=src)
             else:
                 nc.scalar.copy(out=dst, in_=src)
 
-        def quantise(i):
-            codes[i] = pieces.tile([P, PIECE], U32, align_bytes=64, name="codes")
-            scales[i] = pieces.tile([P, PIECE], U8, align_bytes=64, name="scales")
-            nc.vector.quantize_mx(
-                out=codes[i][:].bitcast(FP8X4), scales=scales[i][:], in_=grouped[i][:]
-            )
+            codes = pieces.tile([P, PIECE], U32, align_bytes=64, name="codes")
+            scales = pieces.tile([P, PIECE], U8, align_bytes=64, name="scales")
+            nc.vector.quantize_mx(out=codes[:].bitcast(FP8X4), scales=scales[:], in_=grouped[:])
 
-        def multiply(i):
-            acc[i] = sums.tile([TOKENS, PIECE], F32, name="acc", tag="acc")
+            acc = sums.tile([TOKENS, PIECE], F32, name="acc")
             nc.tensor.matmul_mx(
-                out=acc[i][:],
+                out=acc[:],
                 lhsT=hs_codes[:].bitcast(FP8X4),
                 lhsT_scale=hs_scales[:],
-                rhs=codes[i][:].bitcast(FP8X4),
-                rhs_scale=scales[i][:],
+                rhs=codes[:].bitcast(FP8X4),
+                rhs_scale=scales[:],
                 start=True,
                 stop=True,
             )
 
-        def mean_square(i):
             squares = pieces.tile([TOKENS, HEADS_PER_PIECE, ROWS, P // ROWS], F32, name="squares")
             sumsq = pieces.tile([TOKENS, HEADS_PER_PIECE], F32, name="sumsq")
-            acc_heads = acc[i][:].rearrange("t (a h c) -> t h a c", a=ROWS, h=HEADS_PER_PIECE)
+            acc_heads = acc[:].rearrange("t (a h c) -> t h a c", a=ROWS, h=HEADS_PER_PIECE)
             for h in range(HEADS_PER_PIECE):
                 nc.scalar.activation(
                     out=squares[:, h],
@@ -151,42 +127,25 @@ def tile_combcrossattention_pa_s_kernel(tc, hidden_states, Wq, q_norm_w, out):
                     func=ACT.Square,
                     accum_out=sumsq[:, h : h + 1],
                 )
-            rms = pieces.tile([TOKENS, HEADS_PER_PIECE], F32, name="rms")
+            inv_rms = pieces.tile([TOKENS, HEADS_PER_PIECE], F32, name="inv_rms")
             nc.scalar.activation(
-                out=rms[:], in_=sumsq[:], func=ACT.Sqrt, scale=1.0 / HEAD_DIM, bias=EPS
+                out=inv_rms[:],
+                in_=sumsq[:],
+                func=ACT.Abs_reciprocal_sqrt,
+                scale=1.0 / HEAD_DIM,
+                bias=EPS,
             )
-            return rms
 
-        def normalise(i, rms):
-            inv_rms[i] = pieces.tile([TOKENS, HEADS_PER_PIECE], F32, name="inv_rms")
-            nc.vector.reciprocal(out=inv_rms[i][:], in_=rms[:])
             normed = pieces.tile([TOKENS, HEADS_PER_PIECE, HEAD_DIM], F32, name="normed")
-            acc_by_d = acc[i][:].rearrange("t (a h c) -> t h c a", a=ROWS, h=HEADS_PER_PIECE)
+            acc_by_d = acc[:].rearrange("t (a h c) -> t h c a", a=ROWS, h=HEADS_PER_PIECE)
             for h in range(HEADS_PER_PIECE):
                 nc.vector.scalar_tensor_tensor(
                     out=normed[:, h, :].rearrange("t (c a) -> t c a", a=ROWS),
                     in0=acc_by_d[:, h],
-                    scalar=inv_rms[i][:, h : h + 1],
+                    scalar=inv_rms[:, h : h + 1],
                     in1=gain[:].rearrange("t (c a) -> t c a", a=ROWS),
                     op0=ALU.mult,
                     op1=ALU.mult,
                 )
             heads = out[i * HEADS_PER_PIECE : (i + 1) * HEADS_PER_PIECE]
             nc.sync.dma_start(out=heads.rearrange("h t d -> t h d"), in_=normed[:])
-
-        rms_of = {}
-        for step in range(N_PIECES + 4):
-            if step < N_PIECES:
-                flip(step)
-            if step == 3:
-                spread_gain()
-            if 0 <= step - 1 < N_PIECES:
-                regroup(step - 1)
-            if 0 <= step - 4 < N_PIECES:
-                normalise(step - 4, rms_of[step - 4])
-            if 0 <= step - 1 < N_PIECES:
-                quantise(step - 1)
-            if 0 <= step - 2 < N_PIECES:
-                multiply(step - 2)
-            if 0 <= step - 3 < N_PIECES:
-                rms_of[step - 3] = mean_square(step - 3)

from contextlib import ExitStack

import concourse.masks as masks
import concourse.mybir as mybir

F32 = mybir.dt.float32
BF16 = mybir.dt.bfloat16
U32 = mybir.dt.uint32
U8 = mybir.dt.uint8
FP8X4 = mybir.dt.float8_e4m3fn_x4
ACT = mybir.ActivationFunctionType
ALU = mybir.AluOpType

P = 128
TOKENS = 128
K = 512
HEADS = 16
HEAD_DIM = 128
EPS = 1e-05

K_WORDS = K // 2
HALVES = K_WORDS // P
PACK = 4
PIECE = 256
N_PIECES = HEADS * HEAD_DIM // PIECE
ROWS = PIECE // P
HEADS_PER_PIECE = PIECE // HEAD_DIM
VECTOR_EVERY = 3

FLOPS = 2 * TOKENS * HEADS * HEAD_DIM * K


def tile_combcrossattention_pa_s_kernel(tc, hidden_states, Wq, q_norm_w, out):
    nc = tc.nc
    with ExitStack() as ctx:
        consts = ctx.enter_context(tc.tile_pool(name="consts", bufs=1))
        pieces = ctx.enter_context(tc.tile_pool(name="pieces", bufs=N_PIECES))
        flipped = ctx.enter_context(tc.psum_pool(name="flipped", bufs=4))
        sums = ctx.enter_context(tc.psum_pool(name="sums", bufs=4))

        def load_piece(i):
            raw = pieces.tile([P, ROWS * K], BF16, name="w_raw")
            rows = Wq[i * PIECE : (i + 1) * PIECE, :]
            nc.sync.dma_start(out=raw[:], in_=rows.rearrange("(p a) k -> p (a k)", a=ROWS))
            return raw

        w_raw = [load_piece(0)]
        hs_raw = consts.tile([P, K], BF16)
        nc.sync.dma_start(out=hs_raw[:], in_=hidden_states)
        gain_row = consts.tile([P, HEAD_DIM], BF16)
        nc.vector.memset(gain_row[:], 0.0)
        nc.sync.dma_start(out=gain_row[0:1, :], in_=q_norm_w.rearrange("(o d) -> o d", o=1))
        for i in range(1, N_PIECES):
            w_raw.append(load_piece(i))

        ident = consts.tile([P, P], F32)
        masks.make_identity(nc, ident[:])
        ones = consts.tile([P, P], BF16)
        nc.vector.memset(ones[:], 1.0)
        one = consts.tile([P, 1], F32)
        nc.vector.memset(one[:], 1.0)
        nc.scalar.activation(out=one[:], in_=one[:], func=ACT.Abs_reciprocal_sqrt)

        def transpose_words(dst, src_words):
            for u in range(HALVES):
                nc.tensor.transpose(dst[:, u, :], src_words[:, u * P : (u + 1) * P], ident[:])

        def flip(i):
            words = w_raw[i][:].bitcast(F32)
            bank = flipped.tile([P, ROWS, HALVES, P], F32, name="bank", tag="bank")
            for a in range(ROWS):
                transpose_words(bank[:, a], words[:, a * K_WORDS : (a + 1) * K_WORDS])
            return bank

        bank_of = {0: flip(0)}

        hs_flipped = flipped.tile([P, HALVES, TOKENS], F32, name="hs_flipped", tag="bank")
        transpose_words(hs_flipped, hs_raw[:].bitcast(F32))
        hs_grouped = consts.tile([P, TOKENS * PACK], BF16, align_bytes=64)
        nc.vector.tensor_copy(
            out=hs_grouped[:].bitcast(F32).rearrange("p (r u) -> p r u", u=HALVES),
            in_=hs_flipped[:].rearrange("p u r -> p r u"),
        )
        hs_codes = consts.tile([P, TOKENS], U32, align_bytes=64)
        hs_scales = consts.tile([P, TOKENS], U8, align_bytes=64)
        nc.vector.quantize_mx(out=hs_codes[:].bitcast(FP8X4), scales=hs_scales[:], in_=hs_grouped[:])

        gain_spread = flipped.tile([P, HEAD_DIM], F32, name="gain_spread", tag="bank")
        nc.tensor.matmul(out=gain_spread[:], lhsT=ones[:], rhs=gain_row[:], start=True, stop=True)
        gain = consts.tile([P, HEAD_DIM], F32)
        nc.vector.tensor_copy(out=gain[:], in_=gain_spread[:])

        for i in range(N_PIECES):
            if i + 1 < N_PIECES:
                bank_of[i + 1] = flip(i + 1)

            grouped = pieces.tile([P, PIECE * PACK], BF16, align_bytes=64, name="grouped")
            dst = grouped[:].bitcast(F32).rearrange("p (a c u) -> p a c u", a=ROWS, u=HALVES)
            src = bank_of[i][:].rearrange("p a u c -> p a c u")
            if i % VECTOR_EVERY == 1:
                nc.vector.tensor_copy(out=dst, in_=src)
            else:
                nc.scalar.copy(out=dst, in_=src)

            codes = pieces.tile([P, PIECE], U32, align_bytes=64, name="codes")
            scales = pieces.tile([P, PIECE], U8, align_bytes=64, name="scales")
            nc.vector.quantize_mx(out=codes[:].bitcast(FP8X4), scales=scales[:], in_=grouped[:])

            acc = sums.tile([TOKENS, PIECE], F32, name="acc")
            nc.tensor.matmul_mx(
                out=acc[:],
                lhsT=hs_codes[:].bitcast(FP8X4),
                lhsT_scale=hs_scales[:],
                rhs=codes[:].bitcast(FP8X4),
                rhs_scale=scales[:],
                start=True,
                stop=True,
            )

            squares = pieces.tile([TOKENS, HEADS_PER_PIECE, ROWS, P // ROWS], F32, name="squares")
            sumsq = pieces.tile([TOKENS, HEADS_PER_PIECE], F32, name="sumsq")
            acc_heads = acc[:].rearrange("t (a h c) -> t h a c", a=ROWS, h=HEADS_PER_PIECE)
            for h in range(HEADS_PER_PIECE):
                nc.scalar.activation(
                    out=squares[:, h],
                    in_=acc_heads[:, h],
                    func=ACT.Square,
                    accum_out=sumsq[:, h : h + 1],
                )
            inv_rms = pieces.tile([TOKENS, HEADS_PER_PIECE], F32, name="inv_rms")
            nc.scalar.activation(
                out=inv_rms[:],
                in_=sumsq[:],
                func=ACT.Abs_reciprocal_sqrt,
                scale=1.0 / HEAD_DIM,
                bias=EPS,
            )

            normed = pieces.tile([TOKENS, HEADS_PER_PIECE, HEAD_DIM], F32, name="normed")
            acc_by_d = acc[:].rearrange("t (a h c) -> t h c a", a=ROWS, h=HEADS_PER_PIECE)
            for h in range(HEADS_PER_PIECE):
                nc.vector.scalar_tensor_tensor(
                    out=normed[:, h, :].rearrange("t (c a) -> t c a", a=ROWS),
                    in0=acc_by_d[:, h],
                    scalar=inv_rms[:, h : h + 1],
                    in1=gain[:].rearrange("t (c a) -> t c a", a=ROWS),
                    op0=ALU.mult,
                    op1=ALU.mult,
                )
            heads = out[i * HEADS_PER_PIECE : (i + 1) * HEADS_PER_PIECE]
            nc.sync.dma_start(out=heads.rearrange("h t d -> t h d"), in_=normed[:])
